import numpy as np
import ml_dtypes


def mxq(x, axis, fmt="e4m3"):
    dtype, down = {"e4m3": (ml_dtypes.float8_e4m3fn, 7), "e5m2": (ml_dtypes.float8_e5m2, 14)}[fmt]
    v = np.moveaxis(np.asarray(x, np.float32).astype(ml_dtypes.bfloat16).astype(np.float64), axis, -1)
    blocks = v.reshape(v.shape[:-1] + (-1, 32))
    amax = np.abs(blocks).max(-1, keepdims=True)
    byte = np.maximum(np.where(amax > 0, np.frexp(amax)[1] - 1 + 127, 0) - down, 1)
    scale = np.exp2(byte - 127.0)
    codes = (blocks / scale).astype(np.float32).astype(dtype).astype(np.float64)
    return np.moveaxis((codes * scale).reshape(v.shape), -1, axis)


WIDE = False


def mx_kscale(k):
    if not WIDE:
        return np.ones(k)
    levels = np.array([30, -30])
    if k % 512:
        return np.exp2(np.random.permutation(np.resize(levels, k // 32))).repeat(32)
    a = np.empty((k // 512, 16))
    for p in range(k // 512):
        a[p, :8] = np.random.permutation(np.resize(levels, 8))
        for g in range(8):
            far = levels[np.abs(levels - a[p, g]) >= 10]
            a[p, g + 8] = far[np.random.randint(len(far))]
    return np.exp2(a.ravel()).repeat(32)


BF16 = ml_dtypes.bfloat16


def bf(x):
    return np.asarray(x, np.float32).astype(BF16)


def f64(x):
    return np.asarray(x).astype(np.float64)


E2M1 = np.array([0.0, 0.5, 1.0, 1.5, 2.0, 3.0, 4.0, 6.0, -0.0, -0.5, -1.0, -1.5, -2.0, -3.0, -4.0, -6.0])


def pack_weight(w, fmt):
    k, n = w.shape
    w = f64(bf(w)).reshape(k // 32, 32, n)
    amax = np.abs(w).max(1)
    if fmt == "e4m3":
        byte = np.frexp(amax)[1] - 1 + 127 - 7
    else:
        mant, ex = np.frexp(amax / 6.0)
        byte = np.where(mant > 0.5, ex, ex - 1) + 127
    byte = np.clip(np.where(amax > 0, byte, 1), 1, 254)
    scaled = (w * np.exp2(127.0 - byte)[:, None, :]).reshape(k, n).astype(np.float32)
    by_word = np.ascontiguousarray(scaled.reshape(k // 512, 128, 4, n).transpose(0, 1, 3, 2))
    if fmt == "e4m3":
        words = by_word.astype(ml_dtypes.float8_e4m3fn).view(np.uint8)
    else:
        c = by_word.astype(ml_dtypes.float4_e2m1fn).view(np.uint8) & 0xF
        words = c[..., 0::2] | (c[..., 1::2] << 4)
    return np.ascontiguousarray(words), np.ascontiguousarray(byte.astype(np.uint8).reshape(k // 512, 16, n))


def unpack_weight(words, scales, fmt):
    g, p, n, _ = words.shape
    if fmt == "e4m3":
        vals = np.ascontiguousarray(words).view(ml_dtypes.float8_e4m3fn).astype(np.float64)
    else:
        nib = np.empty((g, p, n, 4), np.uint8)
        nib[..., 0::2] = words & 0xF
        nib[..., 1::2] = words >> 4
        vals = E2M1[nib]
    vals = vals * np.repeat(np.exp2(scales.astype(np.float64) - 127.0), 8, axis=1)[..., None]
    return vals.transpose(0, 1, 3, 2).reshape(g * 512, n)

def pack4(w):
    words, scales = pack_weight(w, "e2m1")
    return words.reshape(words.shape[0], 128, -1), scales


def unpack4(words, scales):
    return unpack_weight(words.reshape(words.shape[0], 128, -1, 2), scales, "e2m1")


B, C, H, W = 2, 1024, 32, 32
C2 = C + C


def setup_inputs():
    s = mx_kscale(C)
    x = bf(np.random.standard_normal((B, C, H, W)) * s[None, :, None, None])
    mask = bf(np.random.random_sample((B, 1, H, W)))
    words, scales = pack4(np.random.standard_normal((C, C2)) / np.sqrt(C) / s[:, None])
    b_kv = bf(np.random.standard_normal(C2) * 0.3)
    return {"x": x,
            "mask": mask,
            "W_kv_words": words,
            "W_kv_scales": scales,
            "b_kv": b_kv}


def reference(x, mask, W_kv_words, W_kv_scales, b_kv):
    x, mask = f64(x), f64(mask)
    b, c, h, w = x.shape
    xf = np.transpose(x, (0, 2, 3, 1)).reshape(b, h * w, c)
    kv = (mxq(xf, 2, "e5m2") @ unpack4(W_kv_words, W_kv_scales)) + f64(b_kv)
    k, v = kv[..., :c], kv[..., c:]
    k = k / np.linalg.norm(k, axis=-1, keepdims=True)
    m = np.transpose(mask, (0, 2, 3, 1)).reshape(b, h * w, 1)
    inv = 1.0 - m
    ku = k * inv
    km = k * m
    kv_know = np.sum(ku * v, axis=-2, keepdims=True)
    kv_mask = np.sum(km * v, axis=-2, keepdims=True)
    return kv_know, kv_mask

@@ -1,0 +1,215 @@
+from contextlib import ExitStack
+
+import concourse.mybir as mybir
+from concourse.masks import make_identity
+
+B, C, T = 2, 1024, 1024
+C2 = 2 * C
+FLOPS = 2 * B * T * C * C2
+
+F32 = mybir.dt.float32
+BF16 = mybir.dt.bfloat16
+I32 = mybir.dt.int32
+U32 = mybir.dt.uint32
+U8 = mybir.dt.uint8
+E5M2X4 = mybir.dt.float8_e5m2_x4
+E2M1X4 = mybir.dt.float4_e2m1fn_x4
+ACT = mybir.ActivationFunctionType
+ALU = mybir.AluOpType
+
+P = 128
+PACK = 4
+PASSES = C // (P * PACK)
+BANK = 512
+BANKS = C2 // BANK
+TILES = B * T // P
+PAIR = 2 * P
+PAIRS = TILES // 2
+CHUNKS = C // P
+LAG = 2
+LOADS = [(0, 0, 256), (0, 256, 512), (0, 512, 1024), (1, 0, 512), (1, 512, 1024)]
+
+
+def tile_hydraattention_pa_kernel(tc, x, mask, W_kv_words, W_kv_scales, b_kv, out_0, out_1):
+    nc = tc.nc
+    with ExitStack() as ctx:
+        keep = ctx.enter_context(tc.tile_pool(name="keep", bufs=1))
+        work = ctx.enter_context(tc.tile_pool(name="work", bufs=3))
+        small = ctx.enter_context(tc.tile_pool(name="small", bufs=4))
+        psum = ctx.enter_context(tc.psum_pool(name="psum", bufs=1))
+        ctx.enter_context(tc.manual_schedule())
+
+        rows = keep.tile([P, BANK], BF16, name="rows")
+        w_scales = keep.tile([P, PASSES, C2], U8, name="w_scales", align_bytes=64)
+        nc.vector.memset(rows[:].bitcast(I32), 0)
+        nc.vector.memset(w_scales[:].rearrange("p g n -> p (g n)").bitcast(I32), 0)
+        ident = keep.tile([P, P], BF16, name="ident")
+        make_identity(nc, ident[:])
+        ident32 = keep.tile([P, P], F32, name="ident32")
+        make_identity(nc, ident32[:])
+        pooled = keep.tile([P, P], F32, name="pooled")
+        nc.gpsimd.memset(pooled[:], 0.0)
+        minus_half = keep.tile([P, 1], F32, name="minus_half")
+        nc.gpsimd.memset(minus_half[:], -0.5)
+
+        nc.scalar.dma_start(out=rows[0:BANKS, :], in_=b_kv.rearrange("(r n) -> r n", r=BANKS))
+        nc.scalar.dma_start(
+            out=rows[BANKS : BANKS + TILES, 0:P],
+            in_=mask.rearrange("b o h w -> (b o h w)").rearrange("(r n) -> r n", n=P),
+        )
+
+        raw = {}
+
+        def load_x(n):
+            b, t0, t1 = LOADS[n]
+            src = x[b].rearrange("(g p j) h w -> g p j (h w)", g=PASSES, j=PACK)
+            for g in range(PASSES):
+                tile = keep.tile([P, PACK, t1 - t0], BF16, name="raw_%d_%d" % (n, g))
+                nc.sync.dma_start(out=tile[:], in_=src[g][:, :, t0:t1])
+                for t in range(t0, t1, P):
+                    raw[((b * T + t) // P, g)] = (tile, t - t0)
+
+        w_words = []
+
+        def load_w(n):
+            tile = keep.tile([P, PASSES, 2 * BANK], U8, name="w_words_%d" % n, align_bytes=64)
+            src = W_kv_words[:, :, 2 * BANK * n : 2 * BANK * (n + 1)].rearrange("g p n -> p g n")
+            nc.sync.dma_start(out=tile[:].bitcast(I32), in_=src.bitcast(I32))
+            w_words.append(tile)
+
+        load_x(0)
+        for q in range(4):
+            nc.sync.dma_start(
+                out=w_scales[32 * q : 32 * q + 4, :, :].bitcast(I32),
+                in_=W_kv_scales[:, 4 * q : 4 * q + 4, :].rearrange("g r n -> r g n").bitcast(I32),
+            )
+        for n in range(BANKS):
+            load_w(n)
+        for n in range(1, len(LOADS)):
+            load_x(n)
+
+        grouped = {}
+        x_mx = {}
+
+        def interleave(copy, first, count, g):
+            tile, t0 = raw[(first, g)]
+            dst = work.tile([P, count * P, PACK], BF16, name="grouped", tag="grouped", align_bytes=64)
+            copy(out=dst[:], in_=tile[:, :, t0 : t0 + count * P].rearrange("p j t -> p t j"))
+            grouped[(first, g)] = (dst, count)
+
+        def quantize(first, g):
+            src, count = grouped[(first, g)]
+            codes = keep.tile([P, count * P], U32, name="codes_%d_%d" % (first, g), align_bytes=64)
+            scales = keep.tile([P, count * P], U8, name="scales_%d_%d" % (first, g), align_bytes=64)
+            nc.vector.quantize_mx(
+                out=codes[:].bitcast(E5M2X4), scales=scales[:], in_=src[:].rearrange("p t j -> p (t j)")
+            )
+            for n in range(count):
+                x_mx[(first + n, g)] = (codes[:, n * P : (n + 1) * P], scales[:, n * P : (n + 1) * P])
+
+        bias = []
+        for n in range(BANKS):
+            spread = psum.tile([P, BANK], F32, name="spread", tag="acc", bufs=7)
+            nc.tensor.matmul(
+                out=spread[:], lhsT=ident[:, n : n + 1].to_broadcast([P, P]), rhs=rows[:], start=True, stop=True
+            )
+            tile = keep.tile([P, BANK], F32, name="bias_%d" % n)
+            nc.scalar.copy(out=tile[:], in_=spread[:])
+            bias.append(tile)
+        turned = psum.tile([P, BANK], F32, name="turned", tag="acc", bufs=7)
+        nc.tensor.matmul(
+            out=turned[:, 0:TILES], lhsT=rows[:, 0:P], rhs=ident[:, BANKS : BANKS + TILES], start=True, stop=True
+        )
+
+        interleave(nc.vector.tensor_copy, 0, 1, 0)
+        interleave(nc.vector.tensor_copy, 0, 1, 1)
+        quantize(0, 0)
+        interleave(nc.vector.tensor_copy, 1, 1, 0)
+        quantize(0, 1)
+        interleave(nc.vector.tensor_copy, 1, 1, 1)
+        quantize(1, 0)
+        gates = keep.tile([P, TILES, 2], F32, name="gates")
+        nc.vector.tensor_scalar(
+            out=gates[:, :, 0], in0=turned[:, 0:TILES], scalar1=-1.0, scalar2=1.0, op0=ALU.mult, op1=ALU.add
+        )
+        quantize(1, 1)
+        nc.vector.tensor_copy(out=gates[:, :, 1], in_=turned[:, 0:TILES])
+
+        units = [(2 * q, g) for q in range(1, PAIRS) for g in range(PASSES)]
+        interleave(nc.scalar.copy, units[0][0], 2, units[0][1])
+
+        sums = psum.tile([P, 2 * B * CHUNKS], F32, name="sums")
+        prod = {}
+        weights = {}
+        inv_norm = {}
+
+        def pool(i, chunks):
+            for j in chunks:
+                col = 2 * ((i // (TILES // B)) * CHUNKS + j)
+                nc.tensor.matmul(
+                    out=sums[:, col : col + 2],
+                    lhsT=prod[i][:, j * P : (j + 1) * P],
+                    rhs=weights[i][:],
+                    start=(i == 0 and j == 0),
+                    stop=(i == TILES - 1 and j == CHUNKS - 1),
+                )
+
+        def weigh(i):
+            weights[i] = small.tile([P, 2], F32, name="weights")
+            nc.scalar.activation(out=weights[i][:], in_=gates[:, i, :], func=ACT.Copy, scale=inv_norm[i][:])
+
+        for i in range(TILES):
+            last = i == TILES - 1
+            keys = work.tile([P, C], F32, name="keys")
+            values = work.tile([P, C], F32, name="values")
+            prod[i] = work.tile([P, C], F32, name="prod", bufs=4)
+            if i + 1 < len(units):
+                interleave(nc.scalar.copy, units[i + 1][0], 2, units[i + 1][1])
+            if i > 0:
+                weigh(i - 1)
+            for n in range(BANKS):
+                acc = psum.tile([P, BANK], F32, name="acc", tag="acc", bufs=7)
+                for g in range(PASSES):
+                    codes, scales = x_mx[(i, g)]
+                    nc.tensor.matmul_mx(
+                        out=acc[:],
+                        lhsT=codes.bitcast(E5M2X4),
+                        lhsT_scale=scales,
+                        rhs=w_words[n][:, g, :].bitcast(E2M1X4),
+                        rhs_scale=w_scales[:, g, BANK * n : BANK * (n + 1)],
+                        start=(g == 0),
+                        stop=(g == PASSES - 1),
+                    )
+                if i >= LAG:
+                    pool(i - LAG, range(2 * n, 2 * n + 2))
+                half = slice((n % 2) * BANK, (n % 2 + 1) * BANK)
+                dst = keys if n < 2 else values
+                nc.vector.tensor_tensor(out=dst[:, half], in0=acc[:], in1=bias[n][:], op=ALU.add)
+                if n == 1:
+                    squares = work.tile([P, C], BF16, name="squares", bufs=2)
+                    norm2 = small.tile([P, 1], F32, name="norm2")
+                    nc.scalar.activation(out=squares[:], in_=keys[:], func=ACT.Square, accum_out=norm2[:])
+                    if i < len(units):
+                        quantize(*units[i])
+                if n == 2:
+                    nc.gpsimd.tensor_tensor(out=prod[i][:, half], in0=keys[:, half], in1=values[:, half], op=ALU.mult)
+                    inv_norm[i] = small.tile([P, 1], F32, name="inv_norm")
+                    nc.gpsimd.tensor_tensor(out=inv_norm[i][:], in0=norm2[:], in1=minus_half[:], op=ALU.pow)
+                if n == 3:
+                    engine = nc.vector if last else nc.gpsimd
+                    engine.tensor_tensor(out=prod[i][:, half], in0=keys[:, half], in1=values[:, half], op=ALU.mult)
+        weigh(TILES - 1)
+        for i in range(TILES - LAG, TILES):
+            pool(i, range(CHUNKS))
+
+        nc.vector.tensor_copy(
+            out=pooled[:, 0 : 2 * B * CHUNKS].rearrange("p (s c) -> p s c", s=2),
+            in_=sums[:].rearrange("p (c s) -> p s c", s=2),
+        )
+        flipped = psum.tile([P, BANK], F32, name="flipped", tag="acc", bufs=7)
+        nc.tensor.transpose(flipped[:, 0:P], pooled[:], ident32[:])
+        result = keep.tile([2 * B * CHUNKS, P], F32, name="result")
+        nc.scalar.copy(out=result[:], in_=flipped[0 : 2 * B * CHUNKS, 0:P])
+        rows_out = B * CHUNKS
+        nc.sync.dma_start(out=out_0.rearrange("b o (j p) -> (b o j) p", p=P), in_=result[0:rows_out, :])
+        nc.scalar.dma_start(out=out_1.rearrange("b o (j p) -> (b o j) p", p=P), in_=result[rows_out : 2 * rows_out, :])

@@ -41,7 +41,7 @@ def tile_hydraattention_pa_kernel(tc, x, mask, W_kv_words, W_kv_scales, b_kv, ou
 
         rows = keep.tile([P, BANK], BF16, name="rows")
         w_scales = keep.tile([P, PASSES, C2], U8, name="w_scales", align_bytes=64)
-        nc.vector.memset(rows[:].bitcast(I32), 0)
+        nc.gpsimd.memset(rows[:].bitcast(I32), 0)
         nc.vector.memset(w_scales[:].rearrange("p g n -> p (g n)").bitcast(I32), 0)
         ident = keep.tile([P, P], BF16, name="ident")
         make_identity(nc, ident[:])
@@ -49,8 +49,6 @@ def tile_hydraattention_pa_kernel(tc, x, mask, W_kv_words, W_kv_scales, b_kv, ou
         make_identity(nc, ident32[:])
         pooled = keep.tile([P, P], F32, name="pooled")
         nc.gpsimd.memset(pooled[:], 0.0)
-        minus_half = keep.tile([P, 1], F32, name="minus_half")
-        nc.gpsimd.memset(minus_half[:], -0.5)
 
         nc.scalar.dma_start(out=rows[0:BANKS, :], in_=b_kv.rearrange("(r n) -> r n", r=BANKS))
         nc.scalar.dma_start(
@@ -83,29 +81,34 @@ def tile_hydraattention_pa_kernel(tc, x, mask, W_kv_words, W_kv_scales, b_kv, ou
                 out=w_scales[32 * q : 32 * q + 4, :, :].bitcast(I32),
                 in_=W_kv_scales[:, 4 * q : 4 * q + 4, :].rearrange("g r n -> r g n").bitcast(I32),
             )
-        for n in range(BANKS):
-            load_w(n)
-        for n in range(1, len(LOADS)):
+        load_w(0)
+        load_w(1)
+        load_x(1)
+        load_w(2)
+        load_w(3)
+        for n in range(2, len(LOADS)):
             load_x(n)
 
         grouped = {}
         x_mx = {}
 
         def interleave(copy, first, count, g):
+            if g == 0:
+                grouped[first] = work.tile([P, PASSES, count * P, PACK], BF16, name="grouped", align_bytes=64)
             tile, t0 = raw[(first, g)]
-            dst = work.tile([P, count * P, PACK], BF16, name="grouped", tag="grouped", align_bytes=64)
-            copy(out=dst[:], in_=tile[:, :, t0 : t0 + count * P].rearrange("p j t -> p t j"))
-            grouped[(first, g)] = (dst, count)
+            copy(out=grouped[first][:, g, :, :], in_=tile[:, :, t0 : t0 + count * P].rearrange("p j t -> p t j"))
 
-        def quantize(first, g):
-            src, count = grouped[(first, g)]
-            codes = keep.tile([P, count * P], U32, name="codes_%d_%d" % (first, g), align_bytes=64)
-            scales = keep.tile([P, count * P], U8, name="scales_%d_%d" % (first, g), align_bytes=64)
+        def quantize(first, count):
+            codes = keep.tile([P, PASSES, count * P], U32, name="codes_%d" % first, align_bytes=64)
+            scales = keep.tile([P, PASSES, count * P], U8, name="scales_%d" % first, align_bytes=64)
             nc.vector.quantize_mx(
-                out=codes[:].bitcast(E5M2X4), scales=scales[:], in_=src[:].rearrange("p t j -> p (t j)")
+                out=codes[:].rearrange("p g t -> p (g t)").bitcast(E5M2X4),
+                scales=scales[:].rearrange("p g t -> p (g t)"),
+                in_=grouped[first][:].rearrange("p g t j -> p (g t j)"),
             )
             for n in range(count):
-                x_mx[(first + n, g)] = (codes[:, n * P : (n + 1) * P], scales[:, n * P : (n + 1) * P])
+                for g in range(PASSES):
+                    x_mx[(first + n, g)] = (codes[:, g, n * P : (n + 1) * P], scales[:, g, n * P : (n + 1) * P])
 
         bias = []
         for n in range(BANKS):
@@ -123,25 +126,21 @@ def tile_hydraattention_pa_kernel(tc, x, mask, W_kv_words, W_kv_scales, b_kv, ou
 
         interleave(nc.vector.tensor_copy, 0, 1, 0)
         interleave(nc.vector.tensor_copy, 0, 1, 1)
-        quantize(0, 0)
         interleave(nc.vector.tensor_copy, 1, 1, 0)
         quantize(0, 1)
         interleave(nc.vector.tensor_copy, 1, 1, 1)
-        quantize(1, 0)
         gates = keep.tile([P, TILES, 2], F32, name="gates")
         nc.vector.tensor_scalar(
             out=gates[:, :, 0], in0=turned[:, 0:TILES], scalar1=-1.0, scalar2=1.0, op0=ALU.mult, op1=ALU.add
         )
         quantize(1, 1)
         nc.vector.tensor_copy(out=gates[:, :, 1], in_=turned[:, 0:TILES])
-
-        units = [(2 * q, g) for q in range(1, PAIRS) for g in range(PASSES)]
-        interleave(nc.scalar.copy, units[0][0], 2, units[0][1])
+        interleave(nc.scalar.copy, 2, 2, 0)
+        interleave(nc.scalar.copy, 2, 2, 1)
 
         sums = psum.tile([P, 2 * B * CHUNKS], F32, name="sums")
         prod = {}
         weights = {}
-        inv_norm = {}
 
         def pool(i, chunks):
             for j in chunks:
@@ -154,19 +153,18 @@ def tile_hydraattention_pa_kernel(tc, x, mask, W_kv_words, W_kv_scales, b_kv, ou
                     stop=(i == TILES - 1 and j == CHUNKS - 1),
                 )
 
+        norms = {}
+
         def weigh(i):
+            inv_norm = small.tile([P, 1], F32, name="inv_norm")
+            nc.vector.reciprocal(out=inv_norm[:], in_=norms[i][:])
             weights[i] = small.tile([P, 2], F32, name="weights")
-            nc.scalar.activation(out=weights[i][:], in_=gates[:, i, :], func=ACT.Copy, scale=inv_norm[i][:])
+            nc.scalar.activation(out=weights[i][:], in_=gates[:, i, :], func=ACT.Copy, scale=inv_norm[:])
 
         for i in range(TILES):
-            last = i == TILES - 1
             keys = work.tile([P, C], F32, name="keys")
             values = work.tile([P, C], F32, name="values")
             prod[i] = work.tile([P, C], F32, name="prod", bufs=4)
-            if i + 1 < len(units):
-                interleave(nc.scalar.copy, units[i + 1][0], 2, units[i + 1][1])
-            if i > 0:
-                weigh(i - 1)
             for n in range(BANKS):
                 acc = psum.tile([P, BANK], F32, name="acc", tag="acc", bufs=7)
                 for g in range(PASSES):
@@ -180,25 +178,30 @@ def tile_hydraattention_pa_kernel(tc, x, mask, W_kv_words, W_kv_scales, b_kv, ou
                         start=(g == 0),
                         stop=(g == PASSES - 1),
                     )
-                if i >= LAG:
-                    pool(i - LAG, range(2 * n, 2 * n + 2))
+                if i >= LAG and n % 2 == 1:
+                    pool(i - LAG, range(2 * n - 2, 2 * n + 2))
                 half = slice((n % 2) * BANK, (n % 2 + 1) * BANK)
                 dst = keys if n < 2 else values
                 nc.vector.tensor_tensor(out=dst[:, half], in0=acc[:], in1=bias[n][:], op=ALU.add)
+                if n == 0 and i > 0:
+                    weigh(i - 1)
                 if n == 1:
                     squares = work.tile([P, C], BF16, name="squares", bufs=2)
                     norm2 = small.tile([P, 1], F32, name="norm2")
+                    norms[i] = small.tile([P, 1], F32, name="norm")
                     nc.scalar.activation(out=squares[:], in_=keys[:], func=ACT.Square, accum_out=norm2[:])
-                    if i < len(units):
-                        quantize(*units[i])
-                if n == 2:
-                    nc.gpsimd.tensor_tensor(out=prod[i][:, half], in0=keys[:, half], in1=values[:, half], op=ALU.mult)
-                    inv_norm[i] = small.tile([P, 1], F32, name="inv_norm")
-                    nc.gpsimd.tensor_tensor(out=inv_norm[i][:], in0=norm2[:], in1=minus_half[:], op=ALU.pow)
-                if n == 3:
-                    engine = nc.vector if last else nc.gpsimd
-                    engine.tensor_tensor(out=prod[i][:, half], in0=keys[:, half], in1=values[:, half], op=ALU.mult)
-        weigh(TILES - 1)
+                    nc.scalar.activation(out=norms[i][:], in_=norm2[:], func=ACT.Sqrt)
+                if n == 2 and i % 2 == 0 and i + 2 < TILES:
+                    quantize(i + 2, 2)
+            if i < TILES - 1:
+                nc.gpsimd.tensor_tensor(out=prod[i][:], in0=keys[:], in1=values[:], op=ALU.mult)
+            else:
+                weigh(i)
+                for half in (slice(0, BANK), slice(BANK, C)):
+                    nc.vector.tensor_tensor(out=prod[i][:, half], in0=keys[:, half], in1=values[:, half], op=ALU.mult)
+            ahead = 2 * (i // 2) + 4
+            if ahead < TILES:
+                interleave(nc.scalar.copy, ahead, 2, i % 2)
         for i in range(TILES - LAG, TILES):
             pool(i, range(CHUNKS))
 

@@ -27,7 +27,11 @@ PAIR = 2 * P
 PAIRS = TILES // 2
 CHUNKS = C // P
 LAG = 2
-LOADS = [(0, 0, 256), (0, 256, 512), (0, 512, 1024), (1, 0, 512), (1, 512, 1024)]
+SLOTS = 4
+PER_IMAGE = TILES // B
+PERIOD, PHASE = 4, 0
+DIRECT = {i for i in range(TILES) if i % PERIOD == PHASE}
+LOADS = [(0, 0, 512), (0, 512, 1024), (1, 0, 512), (1, 512, 1024)]
 
 
 def tile_hydraattention_pa_kernel(tc, x, mask, W_kv_words, W_kv_scales, b_kv, out_0, out_1):
@@ -41,20 +45,22 @@ def tile_hydraattention_pa_kernel(tc, x, mask, W_kv_words, W_kv_scales, b_kv, ou
 
         rows = keep.tile([P, BANK], BF16, name="rows")
         w_scales = keep.tile([P, PASSES, C2], U8, name="w_scales", align_bytes=64)
-        nc.gpsimd.memset(rows[:].bitcast(I32), 0)
+        nc.vector.memset(rows[:].bitcast(I32), 0)
         nc.vector.memset(w_scales[:].rearrange("p g n -> p (g n)").bitcast(I32), 0)
         ident = keep.tile([P, P], BF16, name="ident")
         make_identity(nc, ident[:])
-        ident32 = keep.tile([P, P], F32, name="ident32")
-        make_identity(nc, ident32[:])
-        pooled = keep.tile([P, P], F32, name="pooled")
-        nc.gpsimd.memset(pooled[:], 0.0)
+        mask_rows = keep.tile([P, P], BF16, name="mask_rows")
+        nc.gpsimd.memset(mask_rows[:].bitcast(I32), 0)
+        slots = []
+        for n in range(SLOTS):
+            slot = keep.tile([P, P + 3], F32, name="slot_%d" % n)
+            nc.gpsimd.memset(slot[:], 0.0)
+            slots.append(slot)
+        pick = keep.tile([P, P + 7], F32, name="pick")
+        nc.gpsimd.memset(pick[:], 0.0)
+        nc.gpsimd.memset(pick[:, 7:8], 1.0)
 
-        nc.scalar.dma_start(out=rows[0:BANKS, :], in_=b_kv.rearrange("(r n) -> r n", r=BANKS))
-        nc.scalar.dma_start(
-            out=rows[BANKS : BANKS + TILES, 0:P],
-            in_=mask.rearrange("b o h w -> (b o h w)").rearrange("(r n) -> r n", n=P),
-        )
+        nc.sync.dma_start(out=rows[0:BANKS, :], in_=b_kv.rearrange("(r n) -> r n", r=BANKS))
 
         raw = {}
 
@@ -76,17 +82,19 @@ def tile_hydraattention_pa_kernel(tc, x, mask, W_kv_words, W_kv_scales, b_kv, ou
             w_words.append(tile)
 
         load_x(0)
+        load_w(0)
         for q in range(4):
             nc.sync.dma_start(
                 out=w_scales[32 * q : 32 * q + 4, :, :].bitcast(I32),
                 in_=W_kv_scales[:, 4 * q : 4 * q + 4, :].rearrange("g r n -> r g n").bitcast(I32),
             )
-        load_w(0)
         load_w(1)
-        load_x(1)
         load_w(2)
         load_w(3)
-        for n in range(2, len(LOADS)):
+        nc.sync.dma_start(
+            out=mask_rows[0:TILES, :], in_=mask.rearrange("b o h w -> (b o h w)").rearrange("(r n) -> r n", n=P)
+        )
+        for n in range(1, len(LOADS)):
             load_x(n)
 
         grouped = {}
@@ -111,7 +119,8 @@ def tile_hydraattention_pa_kernel(tc, x, mask, W_kv_words, W_kv_scales, b_kv, ou
                     x_mx[(first + n, g)] = (codes[:, g, n * P : (n + 1) * P], scales[:, g, n * P : (n + 1) * P])
 
         bias = []
-        for n in range(BANKS):
+
+        def spread_bias(n):
             spread = psum.tile([P, BANK], F32, name="spread", tag="acc", bufs=7)
             nc.tensor.matmul(
                 out=spread[:], lhsT=ident[:, n : n + 1].to_broadcast([P, P]), rhs=rows[:], start=True, stop=True
@@ -119,52 +128,92 @@ def tile_hydraattention_pa_kernel(tc, x, mask, W_kv_words, W_kv_scales, b_kv, ou
             tile = keep.tile([P, BANK], F32, name="bias_%d" % n)
             nc.scalar.copy(out=tile[:], in_=spread[:])
             bias.append(tile)
-        turned = psum.tile([P, BANK], F32, name="turned", tag="acc", bufs=7)
-        nc.tensor.matmul(
-            out=turned[:, 0:TILES], lhsT=rows[:, 0:P], rhs=ident[:, BANKS : BANKS + TILES], start=True, stop=True
-        )
+
+        gates = keep.tile([P, TILES, 2], F32, name="gates")
+
+        def turn_mask():
+            turned = psum.tile([P, BANK], F32, name="turned", tag="acc", bufs=7)
+            nc.tensor.matmul(out=turned[:, 0:TILES], lhsT=mask_rows[:], rhs=ident[:, 0:TILES], start=True, stop=True)
+            nc.vector.tensor_scalar(
+                out=gates[:, :, 0], in0=turned[:, 0:TILES], scalar1=-1.0, scalar2=1.0, op0=ALU.mult, op1=ALU.add
+            )
+            nc.vector.tensor_copy(out=gates[:, :, 1], in_=turned[:, 0:TILES])
+
+        spread_bias(0)
+        spread_bias(1)
 
         interleave(nc.vector.tensor_copy, 0, 1, 0)
-        interleave(nc.vector.tensor_copy, 0, 1, 1)
         interleave(nc.vector.tensor_copy, 1, 1, 0)
-        quantize(0, 1)
+        interleave(nc.vector.tensor_copy, 0, 1, 1)
         interleave(nc.vector.tensor_copy, 1, 1, 1)
-        gates = keep.tile([P, TILES, 2], F32, name="gates")
-        nc.vector.tensor_scalar(
-            out=gates[:, :, 0], in0=turned[:, 0:TILES], scalar1=-1.0, scalar2=1.0, op0=ALU.mult, op1=ALU.add
-        )
+        quantize(0, 1)
+        interleave(nc.vector.tensor_copy, 2, 2, 0)
         quantize(1, 1)
-        nc.vector.tensor_copy(out=gates[:, :, 1], in_=turned[:, 0:TILES])
-        interleave(nc.scalar.copy, 2, 2, 0)
         interleave(nc.scalar.copy, 2, 2, 1)
+        spread_bias(2)
+        spread_bias(3)
+        quantize(2, 2)
 
-        sums = psum.tile([P, 2 * B * CHUNKS], F32, name="sums")
-        prod = {}
-        weights = {}
+        sums = psum.tile([P, BANK], F32, name="sums")
+        keys, values, prod, norms, inv_norms, running = {}, {}, {}, {}, {}, {}
+        halves = (slice(0, BANK), slice(BANK, C))
 
-        def pool(i, chunks):
-            for j in chunks:
-                col = 2 * ((i // (TILES // B)) * CHUNKS + j)
-                nc.tensor.matmul(
-                    out=sums[:, col : col + 2],
-                    lhsT=prod[i][:, j * P : (j + 1) * P],
-                    rhs=weights[i][:],
-                    start=(i == 0 and j == 0),
-                    stop=(i == TILES - 1 and j == CHUNKS - 1),
-                )
+        def multiply(engine, i, h, tag, bufs):
+            prod[(i, h)] = work.tile([P, BANK], F32, name=tag, bufs=bufs)
+            engine.tensor_tensor(out=prod[(i, h)][:], in0=keys[i][:, halves[h]], in1=values[i][:, halves[h]], op=ALU.mult)
 
-        norms = {}
+        def weight(i, s):
+            return slots[i % SLOTS][:, 3 + 4 * s : 4 + 4 * s]
 
         def weigh(i):
-            inv_norm = small.tile([P, 1], F32, name="inv_norm")
-            nc.vector.reciprocal(out=inv_norm[:], in_=norms[i][:])
-            weights[i] = small.tile([P, 2], F32, name="weights")
-            nc.scalar.activation(out=weights[i][:], in_=gates[:, i, :], func=ACT.Copy, scale=inv_norm[:])
+            nc.scalar.activation(out=slots[i % SLOTS][:, 3:8:4], in_=gates[:, i, :], func=ACT.Copy, scale=inv_norms[i][:])
+
+        def invert(i):
+            inv_norms[i] = small.tile([P, 1], F32, name="inv_norm")
+            nc.vector.reciprocal(out=inv_norms[i][:], in_=norms[i][:])
+
+        def pool(i, h):
+            first = 3 - (2 * (i // PER_IMAGE) + h)
+            nc.tensor.matmul(
+                out=sums[:],
+                lhsT=slots[i % SLOTS][:, first : first + P],
+                rhs=prod[(i, h)][:],
+                start=(i == 0 and h == int(0 in DIRECT)),
+                stop=False,
+            )
+
+        def accumulate(i):
+            b = i // PER_IMAGE
+            for s in range(2):
+                if (b, s) not in running:
+                    running[(b, s)] = keep.tile([P, BANK], F32, name="running_%d_%d" % (b, s))
+                    nc.vector.tensor_scalar(
+                        out=running[(b, s)][:], in0=prod[(i, 1)][:], scalar1=weight(i, s), scalar2=None, op0=ALU.mult
+                    )
+                else:
+                    nc.vector.scalar_tensor_tensor(
+                        out=running[(b, s)][:],
+                        in0=prod[(i, 1)][:],
+                        scalar=weight(i, s),
+                        in1=running[(b, s)][:],
+                        op0=ALU.mult,
+                        op1=ALU.add,
+                    )
+
+        def pool_running(b):
+            for s in range(2):
+                first = 7 - (4 * s + 2 * b + 1)
+                nc.tensor.matmul(
+                    out=sums[:], lhsT=pick[:, first : first + P], rhs=running[(b, s)][:], start=False, stop=(b == B - 1 and s == 1)
+                )
 
         for i in range(TILES):
-            keys = work.tile([P, C], F32, name="keys")
-            values = work.tile([P, C], F32, name="values")
-            prod[i] = work.tile([P, C], F32, name="prod", bufs=4)
+            if i > 0:
+                multiply(nc.gpsimd, i - 1, 1, "upper_%d" % (len([j for j in DIRECT if j < i - 1]) % 3), 1)
+                multiply(nc.gpsimd, i - 1, 0, "lower", 5)
+                weigh(i - 1)
+            keys[i] = work.tile([P, C], F32, name="keys")
+            values[i] = work.tile([P, C], F32, name="values")
             for n in range(BANKS):
                 acc = psum.tile([P, BANK], F32, name="acc", tag="acc", bufs=7)
                 for g in range(PASSES):
@@ -178,41 +227,44 @@ def tile_hydraattention_pa_kernel(tc, x, mask, W_kv_words, W_kv_scales, b_kv, ou
                         start=(g == 0),
                         stop=(g == PASSES - 1),
                     )
-                if i >= LAG and n % 2 == 1:
-                    pool(i - LAG, range(2 * n - 2, 2 * n + 2))
-                half = slice((n % 2) * BANK, (n % 2 + 1) * BANK)
-                dst = keys if n < 2 else values
-                nc.vector.tensor_tensor(out=dst[:, half], in0=acc[:], in1=bias[n][:], op=ALU.add)
-                if n == 0 and i > 0:
-                    weigh(i - 1)
+                dst = keys[i] if n < 2 else values[i]
+                nc.vector.tensor_tensor(out=dst[:, halves[n % 2]], in0=acc[:], in1=bias[n][:], op=ALU.add)
                 if n == 1:
                     squares = work.tile([P, C], BF16, name="squares", bufs=2)
                     norm2 = small.tile([P, 1], F32, name="norm2")
                     norms[i] = small.tile([P, 1], F32, name="norm")
-                    nc.scalar.activation(out=squares[:], in_=keys[:], func=ACT.Square, accum_out=norm2[:])
+                    nc.scalar.activation(out=squares[:], in_=keys[i][:], func=ACT.Square, accum_out=norm2[:])
                     nc.scalar.activation(out=norms[i][:], in_=norm2[:], func=ACT.Sqrt)
-                if n == 2 and i % 2 == 0 and i + 2 < TILES:
-                    quantize(i + 2, 2)
-            if i < TILES - 1:
-                nc.gpsimd.tensor_tensor(out=prod[i][:], in0=keys[:], in1=values[:], op=ALU.mult)
-            else:
-                weigh(i)
-                for half in (slice(0, BANK), slice(BANK, C)):
-                    nc.vector.tensor_tensor(out=prod[i][:, half], in0=keys[:, half], in1=values[:, half], op=ALU.mult)
             ahead = 2 * (i // 2) + 4
             if ahead < TILES:
                 interleave(nc.scalar.copy, ahead, 2, i % 2)
-        for i in range(TILES - LAG, TILES):
-            pool(i, range(CHUNKS))
+            if i == 0:
+                turn_mask()
+            if i - LAG in DIRECT:
+                pool(i - LAG, 1)
+            if i >= LAG:
+                pool(i - LAG, 0)
+            if i - LAG == PER_IMAGE:
+                pool_running(0)
+            if i % 2 == 0 and 2 < i + 2 < TILES:
+                quantize(i + 2, 2)
+            if i == TILES - 1:
+                multiply(nc.vector, i, 0, "lower", 5)
+                invert(i)
+            if i > 0 and i - 1 not in DIRECT:
+                accumulate(i - 1)
+            if i < TILES - 1:
+                invert(i)
 
-        nc.vector.tensor_copy(
-            out=pooled[:, 0 : 2 * B * CHUNKS].rearrange("p (s c) -> p s c", s=2),
-            in_=sums[:].rearrange("p (c s) -> p s c", s=2),
-        )
-        flipped = psum.tile([P, BANK], F32, name="flipped", tag="acc", bufs=7)
-        nc.tensor.transpose(flipped[:, 0:P], pooled[:], ident32[:])
-        result = keep.tile([2 * B * CHUNKS, P], F32, name="result")
-        nc.scalar.copy(out=result[:], in_=flipped[0 : 2 * B * CHUNKS, 0:P])
-        rows_out = B * CHUNKS
-        nc.sync.dma_start(out=out_0.rearrange("b o (j p) -> (b o j) p", p=P), in_=result[0:rows_out, :])
-        nc.scalar.dma_start(out=out_1.rearrange("b o (j p) -> (b o j) p", p=P), in_=result[rows_out : 2 * rows_out, :])
+        last = TILES - 1
+        weigh(last)
+        multiply(nc.vector, last, 1, "lower", 5)
+        accumulate(last)
+        pool(last - 1, 0)
+        pool(last, 0)
+        pool_running(B - 1)
+
+        result = keep.tile([8, BANK], F32, name="result")
+        nc.vector.tensor_copy(out=result[:], in_=sums[0:8, :])
+        nc.sync.dma_start(out=out_0.rearrange("b o (h n) -> (b o h) n", h=2), in_=result[0:4, :])
+        nc.scalar.dma_start(out=out_1.rearrange("b o (h n) -> (b o h) n", h=2), in_=result[4:8, :])

@@ -29,7 +29,9 @@ CHUNKS = C // P
 LAG = 2
 SLOTS = 4
 PER_IMAGE = TILES // B
-PERIOD, PHASE = 4, 0
+LATE = 32
+SHARE = 64
+PERIOD, PHASE = 6, 1
 DIRECT = {i for i in range(TILES) if i % PERIOD == PHASE}
 LOADS = [(0, 0, 512), (0, 512, 1024), (1, 0, 512), (1, 512, 1024)]
 
@@ -50,17 +52,17 @@ def tile_hydraattention_pa_kernel(tc, x, mask, W_kv_words, W_kv_scales, b_kv, ou
         ident = keep.tile([P, P], BF16, name="ident")
         make_identity(nc, ident[:])
         mask_rows = keep.tile([P, P], BF16, name="mask_rows")
-        nc.gpsimd.memset(mask_rows[:].bitcast(I32), 0)
+        nc.vector.memset(mask_rows[:].bitcast(I32), 0)
         slots = []
         for n in range(SLOTS):
             slot = keep.tile([P, P + 3], F32, name="slot_%d" % n)
-            nc.gpsimd.memset(slot[:], 0.0)
+            nc.vector.memset(slot[:], 0.0)
             slots.append(slot)
         pick = keep.tile([P, P + 7], F32, name="pick")
-        nc.gpsimd.memset(pick[:], 0.0)
-        nc.gpsimd.memset(pick[:, 7:8], 1.0)
+        nc.vector.memset(pick[:], 0.0)
+        nc.vector.memset(pick[:, 7:8], 1.0)
 
-        nc.sync.dma_start(out=rows[0:BANKS, :], in_=b_kv.rearrange("(r n) -> r n", r=BANKS))
+        nc.scalar.dma_start(out=rows[0:BANKS, :], in_=b_kv.rearrange("(r n) -> r n", r=BANKS))
 
         raw = {}
 
@@ -82,12 +84,12 @@ def tile_hydraattention_pa_kernel(tc, x, mask, W_kv_words, W_kv_scales, b_kv, ou
             w_words.append(tile)
 
         load_x(0)
-        load_w(0)
-        for q in range(4):
+        for r in range(4):
             nc.sync.dma_start(
-                out=w_scales[32 * q : 32 * q + 4, :, :].bitcast(I32),
-                in_=W_kv_scales[:, 4 * q : 4 * q + 4, :].rearrange("g r n -> r g n").bitcast(I32),
+                out=w_scales[r:P:32, :, :].bitcast(I32),
+                in_=W_kv_scales[:, r:16:4, :].rearrange("g q n -> q g n").bitcast(I32),
             )
+        load_w(0)
         load_w(1)
         load_w(2)
         load_w(3)
@@ -126,7 +128,7 @@ def tile_hydraattention_pa_kernel(tc, x, mask, W_kv_words, W_kv_scales, b_kv, ou
                 out=spread[:], lhsT=ident[:, n : n + 1].to_broadcast([P, P]), rhs=rows[:], start=True, stop=True
             )
             tile = keep.tile([P, BANK], F32, name="bias_%d" % n)
-            nc.scalar.copy(out=tile[:], in_=spread[:])
+            nc.scalar.activation(out=tile[:], in_=spread[:], func=ACT.Copy)
             bias.append(tile)
 
         gates = keep.tile([P, TILES, 2], F32, name="gates")
@@ -139,28 +141,24 @@ def tile_hydraattention_pa_kernel(tc, x, mask, W_kv_words, W_kv_scales, b_kv, ou
             )
             nc.vector.tensor_copy(out=gates[:, :, 1], in_=turned[:, 0:TILES])
 
-        spread_bias(0)
-        spread_bias(1)
+        for n in range(BANKS):
+            spread_bias(n)
 
         interleave(nc.vector.tensor_copy, 0, 1, 0)
         interleave(nc.vector.tensor_copy, 1, 1, 0)
+        interleave(nc.vector.tensor_copy, 2, 2, 0)
         interleave(nc.vector.tensor_copy, 0, 1, 1)
         interleave(nc.vector.tensor_copy, 1, 1, 1)
         quantize(0, 1)
-        interleave(nc.vector.tensor_copy, 2, 2, 0)
         quantize(1, 1)
         interleave(nc.scalar.copy, 2, 2, 1)
-        spread_bias(2)
-        spread_bias(3)
-        quantize(2, 2)
 
         sums = psum.tile([P, BANK], F32, name="sums")
-        keys, values, prod, norms, inv_norms, running = {}, {}, {}, {}, {}, {}
+        keys, values, prod, inv_norms, running = {}, {}, {}, {}, {}
         halves = (slice(0, BANK), slice(BANK, C))
 
-        def multiply(engine, i, h, tag, bufs):
-            prod[(i, h)] = work.tile([P, BANK], F32, name=tag, bufs=bufs)
-            engine.tensor_tensor(out=prod[(i, h)][:], in0=keys[i][:, halves[h]], in1=values[i][:, halves[h]], op=ALU.mult)
+        def multiply(engine, i, cols):
+            engine.tensor_tensor(out=prod[i][:, cols], in0=keys[i][:, cols], in1=values[i][:, cols], op=ALU.mult)
 
         def weight(i, s):
             return slots[i % SLOTS][:, 3 + 4 * s : 4 + 4 * s]
@@ -168,16 +166,12 @@ def tile_hydraattention_pa_kernel(tc, x, mask, W_kv_words, W_kv_scales, b_kv, ou
         def weigh(i):
             nc.scalar.activation(out=slots[i % SLOTS][:, 3:8:4], in_=gates[:, i, :], func=ACT.Copy, scale=inv_norms[i][:])
 
-        def invert(i):
-            inv_norms[i] = small.tile([P, 1], F32, name="inv_norm")
-            nc.vector.reciprocal(out=inv_norms[i][:], in_=norms[i][:])
-
         def pool(i, h):
             first = 3 - (2 * (i // PER_IMAGE) + h)
             nc.tensor.matmul(
                 out=sums[:],
                 lhsT=slots[i % SLOTS][:, first : first + P],
-                rhs=prod[(i, h)][:],
+                rhs=prod[i][:, halves[h]],
                 start=(i == 0 and h == int(0 in DIRECT)),
                 stop=False,
             )
@@ -187,13 +181,13 @@ def tile_hydraattention_pa_kernel(tc, x, mask, W_kv_words, W_kv_scales, b_kv, ou
             for s in range(2):
                 if (b, s) not in running:
                     running[(b, s)] = keep.tile([P, BANK], F32, name="running_%d_%d" % (b, s))
-                    nc.vector.tensor_scalar(
-                        out=running[(b, s)][:], in0=prod[(i, 1)][:], scalar1=weight(i, s), scalar2=None, op0=ALU.mult
+                    nc.scalar.activation(
+                        out=running[(b, s)][:], in_=prod[i][:, halves[1]], func=ACT.Copy, scale=weight(i, s)
                     )
                 else:
                     nc.vector.scalar_tensor_tensor(
                         out=running[(b, s)][:],
-                        in0=prod[(i, 1)][:],
+                        in0=prod[i][:, halves[1]],
                         scalar=weight(i, s),
                         in1=running[(b, s)][:],
                         op0=ALU.mult,
@@ -208,12 +202,9 @@ def tile_hydraattention_pa_kernel(tc, x, mask, W_kv_words, W_kv_scales, b_kv, ou
                 )
 
         for i in range(TILES):
-            if i > 0:
-                multiply(nc.gpsimd, i - 1, 1, "upper_%d" % (len([j for j in DIRECT if j < i - 1]) % 3), 1)
-                multiply(nc.gpsimd, i - 1, 0, "lower", 5)
-                weigh(i - 1)
             keys[i] = work.tile([P, C], F32, name="keys")
             values[i] = work.tile([P, C], F32, name="values")
+            prod[i] = work.tile([P, C], F32, name="prod", bufs=4)
             for n in range(BANKS):
                 acc = psum.tile([P, BANK], F32, name="acc", tag="acc", bufs=7)
                 for g in range(PASSES):
@@ -227,38 +218,41 @@ def tile_hydraattention_pa_kernel(tc, x, mask, W_kv_words, W_kv_scales, b_kv, ou
                         start=(g == 0),
                         stop=(g == PASSES - 1),
                     )
-                dst = keys[i] if n < 2 else values[i]
-                nc.vector.tensor_tensor(out=dst[:, halves[n % 2]], in0=acc[:], in1=bias[n][:], op=ALU.add)
+                dst = (keys[i] if n < 2 else values[i])[:, halves[n % 2]]
+                early = BANK - LATE if n == BANKS - 1 and i < TILES - 1 else BANK
+                nc.vector.tensor_tensor(out=dst[:, :early], in0=acc[:, :early], in1=bias[n][:, :early], op=ALU.add)
                 if n == 1:
                     squares = work.tile([P, C], BF16, name="squares", bufs=2)
                     norm2 = small.tile([P, 1], F32, name="norm2")
-                    norms[i] = small.tile([P, 1], F32, name="norm")
+                    inv_norms[i] = small.tile([P, 1], F32, name="inv_norm")
                     nc.scalar.activation(out=squares[:], in_=keys[i][:], func=ACT.Square, accum_out=norm2[:])
-                    nc.scalar.activation(out=norms[i][:], in_=norm2[:], func=ACT.Sqrt)
-            ahead = 2 * (i // 2) + 4
-            if ahead < TILES:
-                interleave(nc.scalar.copy, ahead, 2, i % 2)
+                    nc.scalar.activation(out=inv_norms[i][:], in_=norm2[:], func=ACT.Abs_reciprocal_sqrt)
             if i == 0:
                 turn_mask()
+            weigh(i)
             if i - LAG in DIRECT:
                 pool(i - LAG, 1)
             if i >= LAG:
                 pool(i - LAG, 0)
             if i - LAG == PER_IMAGE:
                 pool_running(0)
-            if i % 2 == 0 and 2 < i + 2 < TILES:
+            if i % 2 == 0 and i + 2 < TILES:
                 quantize(i + 2, 2)
             if i == TILES - 1:
-                multiply(nc.vector, i, 0, "lower", 5)
-                invert(i)
+                multiply(nc.vector, i, halves[0])
+            elif SHARE:
+                multiply(nc.vector, i, slice(0, SHARE))
             if i > 0 and i - 1 not in DIRECT:
                 accumulate(i - 1)
+            ahead = 2 * (i // 2) + 4
+            if ahead < TILES:
+                interleave(nc.scalar.copy, ahead, 2, i % 2)
             if i < TILES - 1:
-                invert(i)
+                nc.vector.tensor_tensor(out=dst[:, early:], in0=acc[:, early:], in1=bias[n][:, early:], op=ALU.add)
+                multiply(nc.gpsimd, i, slice(SHARE, C))
 
         last = TILES - 1
-        weigh(last)
-        multiply(nc.vector, last, 1, "lower", 5)
+        multiply(nc.vector, last, halves[1])
         accumulate(last)
         pool(last - 1, 0)
         pool(last, 0)

from contextlib import ExitStack

import concourse.mybir as mybir
from concourse.masks import make_identity

B, C, T = 2, 1024, 1024
C2 = 2 * C
FLOPS = 2 * B * T * C * C2

F32 = mybir.dt.float32
BF16 = mybir.dt.bfloat16
I32 = mybir.dt.int32
U32 = mybir.dt.uint32
U8 = mybir.dt.uint8
E5M2X4 = mybir.dt.float8_e5m2_x4
E2M1X4 = mybir.dt.float4_e2m1fn_x4
ACT = mybir.ActivationFunctionType
ALU = mybir.AluOpType

P = 128
PACK = 4
PASSES = C // (P * PACK)
BANK = 512
BANKS = C2 // BANK
TILES = B * T // P
PAIR = 2 * P
PAIRS = TILES // 2
CHUNKS = C // P
LAG = 2
SLOTS = 4
PER_IMAGE = TILES // B
LATE = 32
SHARE = 64
PERIOD, PHASE = 6, 1
DIRECT = {i for i in range(TILES) if i % PERIOD == PHASE}
LOADS = [(0, 0, 512), (0, 512, 1024), (1, 0, 512), (1, 512, 1024)]


def tile_hydraattention_pa_kernel(tc, x, mask, W_kv_words, W_kv_scales, b_kv, out_0, out_1):
    nc = tc.nc
    with ExitStack() as ctx:
        keep = ctx.enter_context(tc.tile_pool(name="keep", bufs=1))
        work = ctx.enter_context(tc.tile_pool(name="work", bufs=3))
        small = ctx.enter_context(tc.tile_pool(name="small", bufs=4))
        psum = ctx.enter_context(tc.psum_pool(name="psum", bufs=1))
        ctx.enter_context(tc.manual_schedule())

        rows = keep.tile([P, BANK], BF16, name="rows")
        w_scales = keep.tile([P, PASSES, C2], U8, name="w_scales", align_bytes=64)
        nc.vector.memset(rows[:].bitcast(I32), 0)
        nc.vector.memset(w_scales[:].rearrange("p g n -> p (g n)").bitcast(I32), 0)
        ident = keep.tile([P, P], BF16, name="ident")
        make_identity(nc, ident[:])
        mask_rows = keep.tile([P, P], BF16, name="mask_rows")
        nc.vector.memset(mask_rows[:].bitcast(I32), 0)
        slots = []
        for n in range(SLOTS):
            slot = keep.tile([P, P + 3], F32, name="slot_%d" % n)
            nc.vector.memset(slot[:], 0.0)
            slots.append(slot)
        pick = keep.tile([P, P + 7], F32, name="pick")
        nc.vector.memset(pick[:], 0.0)
        nc.vector.memset(pick[:, 7:8], 1.0)

        nc.scalar.dma_start(out=rows[0:BANKS, :], in_=b_kv.rearrange("(r n) -> r n", r=BANKS))

        raw = {}

        def load_x(n):
            b, t0, t1 = LOADS[n]
            src = x[b].rearrange("(g p j) h w -> g p j (h w)", g=PASSES, j=PACK)
            for g in range(PASSES):
                tile = keep.tile([P, PACK, t1 - t0], BF16, name="raw_%d_%d" % (n, g))
                nc.sync.dma_start(out=tile[:], in_=src[g][:, :, t0:t1])
                for t in range(t0, t1, P):
                    raw[((b * T + t) // P, g)] = (tile, t - t0)

        w_words = []

        def load_w(n):
            tile = keep.tile([P, PASSES, 2 * BANK], U8, name="w_words_%d" % n, align_bytes=64)
            src = W_kv_words[:, :, 2 * BANK * n : 2 * BANK * (n + 1)].rearrange("g p n -> p g n")
            nc.sync.dma_start(out=tile[:].bitcast(I32), in_=src.bitcast(I32))
            w_words.append(tile)

        load_x(0)
        for r in range(4):
            nc.sync.dma_start(
                out=w_scales[r:P:32, :, :].bitcast(I32),
                in_=W_kv_scales[:, r:16:4, :].rearrange("g q n -> q g n").bitcast(I32),
            )
        load_w(0)
        load_w(1)
        load_w(2)
        load_w(3)
        nc.sync.dma_start(
            out=mask_rows[0:TILES, :], in_=mask.rearrange("b o h w -> (b o h w)").rearrange("(r n) -> r n", n=P)
        )
        for n in range(1, len(LOADS)):
            load_x(n)

        grouped = {}
        x_mx = {}

        def interleave(copy, first, count, g):
            if g == 0:
                grouped[first] = work.tile([P, PASSES, count * P, PACK], BF16, name="grouped", align_bytes=64)
            tile, t0 = raw[(first, g)]
            copy(out=grouped[first][:, g, :, :], in_=tile[:, :, t0 : t0 + count * P].rearrange("p j t -> p t j"))

        def quantize(first, count):
            codes = keep.tile([P, PASSES, count * P], U32, name="codes_%d" % first, align_bytes=64)
            scales = keep.tile([P, PASSES, count * P], U8, name="scales_%d" % first, align_bytes=64)
            nc.vector.quantize_mx(
                out=codes[:].rearrange("p g t -> p (g t)").bitcast(E5M2X4),
                scales=scales[:].rearrange("p g t -> p (g t)"),
                in_=grouped[first][:].rearrange("p g t j -> p (g t j)"),
            )
            for n in range(count):
                for g in range(PASSES):
                    x_mx[(first + n, g)] = (codes[:, g, n * P : (n + 1) * P], scales[:, g, n * P : (n + 1) * P])

        bias = []

        def spread_bias(n):
            spread = psum.tile([P, BANK], F32, name="spread", tag="acc", bufs=7)
            nc.tensor.matmul(
                out=spread[:], lhsT=ident[:, n : n + 1].to_broadcast([P, P]), rhs=rows[:], start=True, stop=True
            )
            tile = keep.tile([P, BANK], F32, name="bias_%d" % n)
            nc.scalar.activation(out=tile[:], in_=spread[:], func=ACT.Copy)
            bias.append(tile)

        gates = keep.tile([P, TILES, 2], F32, name="gates")

        def turn_mask():
            turned = psum.tile([P, BANK], F32, name="turned", tag="acc", bufs=7)
            nc.tensor.matmul(out=turned[:, 0:TILES], lhsT=mask_rows[:], rhs=ident[:, 0:TILES], start=True, stop=True)
            nc.vector.tensor_scalar(
                out=gates[:, :, 0], in0=turned[:, 0:TILES], scalar1=-1.0, scalar2=1.0, op0=ALU.mult, op1=ALU.add
            )
            nc.vector.tensor_copy(out=gates[:, :, 1], in_=turned[:, 0:TILES])

        for n in range(BANKS):
            spread_bias(n)

        interleave(nc.vector.tensor_copy, 0, 1, 0)
        interleave(nc.vector.tensor_copy, 1, 1, 0)
        interleave(nc.vector.tensor_copy, 2, 2, 0)
        interleave(nc.vector.tensor_copy, 0, 1, 1)
        interleave(nc.vector.tensor_copy, 1, 1, 1)
        quantize(0, 1)
        quantize(1, 1)
        interleave(nc.scalar.copy, 2, 2, 1)

        sums = psum.tile([P, BANK], F32, name="sums")
        keys, values, prod, inv_norms, running = {}, {}, {}, {}, {}
        halves = (slice(0, BANK), slice(BANK, C))

        def multiply(engine, i, cols):
            engine.tensor_tensor(out=prod[i][:, cols], in0=keys[i][:, cols], in1=values[i][:, cols], op=ALU.mult)

        def weight(i, s):
            return slots[i % SLOTS][:, 3 + 4 * s : 4 + 4 * s]

        def weigh(i):
            nc.scalar.activation(out=slots[i % SLOTS][:, 3:8:4], in_=gates[:, i, :], func=ACT.Copy, scale=inv_norms[i][:])

        def pool(i, h):
            first = 3 - (2 * (i // PER_IMAGE) + h)
            nc.tensor.matmul(
                out=sums[:],
                lhsT=slots[i % SLOTS][:, first : first + P],
                rhs=prod[i][:, halves[h]],
                start=(i == 0 and h == int(0 in DIRECT)),
                stop=False,
            )

        def accumulate(i):
            b = i // PER_IMAGE
            for s in range(2):
                if (b, s) not in running:
                    running[(b, s)] = keep.tile([P, BANK], F32, name="running_%d_%d" % (b, s))
                    nc.scalar.activation(
                        out=running[(b, s)][:], in_=prod[i][:, halves[1]], func=ACT.Copy, scale=weight(i, s)
                    )
                else:
                    nc.vector.scalar_tensor_tensor(
                        out=running[(b, s)][:],
                        in0=prod[i][:, halves[1]],
                        scalar=weight(i, s),
                        in1=running[(b, s)][:],
                        op0=ALU.mult,
                        op1=ALU.add,
                    )

        def pool_running(b):
            for s in range(2):
                first = 7 - (4 * s + 2 * b + 1)
                nc.tensor.matmul(
                    out=sums[:], lhsT=pick[:, first : first + P], rhs=running[(b, s)][:], start=False, stop=(b == B - 1 and s == 1)
                )

        for i in range(TILES):
            keys[i] = work.tile([P, C], F32, name="keys")
            values[i] = work.tile([P, C], F32, name="values")
            prod[i] = work.tile([P, C], F32, name="prod", bufs=4)
            for n in range(BANKS):
                acc = psum.tile([P, BANK], F32, name="acc", tag="acc", bufs=7)
                for g in range(PASSES):
                    codes, scales = x_mx[(i, g)]
                    nc.tensor.matmul_mx(
                        out=acc[:],
                        lhsT=codes.bitcast(E5M2X4),
                        lhsT_scale=scales,
                        rhs=w_words[n][:, g, :].bitcast(E2M1X4),
                        rhs_scale=w_scales[:, g, BANK * n : BANK * (n + 1)],
                        start=(g == 0),
                        stop=(g == PASSES - 1),
                    )
                dst = (keys[i] if n < 2 else values[i])[:, halves[n % 2]]
                early = BANK - LATE if n == BANKS - 1 and i < TILES - 1 else BANK
                nc.vector.tensor_tensor(out=dst[:, :early], in0=acc[:, :early], in1=bias[n][:, :early], op=ALU.add)
                if n == 1:
                    squares = work.tile([P, C], BF16, name="squares", bufs=2)
                    norm2 = small.tile([P, 1], F32, name="norm2")
                    inv_norms[i] = small.tile([P, 1], F32, name="inv_norm")
                    nc.scalar.activation(out=squares[:], in_=keys[i][:], func=ACT.Square, accum_out=norm2[:])
                    nc.scalar.activation(out=inv_norms[i][:], in_=norm2[:], func=ACT.Abs_reciprocal_sqrt)
            if i == 0:
                turn_mask()
            weigh(i)
            if i - LAG in DIRECT:
                pool(i - LAG, 1)
            if i >= LAG:
                pool(i - LAG, 0)
            if i - LAG == PER_IMAGE:
                pool_running(0)
            if i % 2 == 0 and i + 2 < TILES:
                quantize(i + 2, 2)
            if i == TILES - 1:
                multiply(nc.vector, i, halves[0])
            elif SHARE:
                multiply(nc.vector, i, slice(0, SHARE))
            if i > 0 and i - 1 not in DIRECT:
                accumulate(i - 1)
            ahead = 2 * (i // 2) + 4
            if ahead < TILES:
                interleave(nc.scalar.copy, ahead, 2, i % 2)
            if i < TILES - 1:
                nc.vector.tensor_tensor(out=dst[:, early:], in0=acc[:, early:], in1=bias[n][:, early:], op=ALU.add)
                multiply(nc.gpsimd, i, slice(SHARE, C))

        last = TILES - 1
        multiply(nc.vector, last, halves[1])
        accumulate(last)
        pool(last - 1, 0)
        pool(last, 0)
        pool_running(B - 1)

        result = keep.tile([8, BANK], F32, name="result")
        nc.vector.tensor_copy(out=result[:], in_=sums[0:8, :])
        nc.sync.dma_start(out=out_0.rearrange("b o (h n) -> (b o h) n", h=2), in_=result[0:4, :])
        nc.scalar.dma_start(out=out_1.rearrange("b o (h n) -> (b o h) n", h=2), in_=result[4:8, :])
